import numpy as np
import ml_dtypes


def mxq(x, axis, fmt="e4m3"):
    dtype, down = {"e4m3": (ml_dtypes.float8_e4m3fn, 7), "e5m2": (ml_dtypes.float8_e5m2, 14)}[fmt]
    v = np.moveaxis(np.asarray(x, np.float32).astype(ml_dtypes.bfloat16).astype(np.float64), axis, -1)
    blocks = v.reshape(v.shape[:-1] + (-1, 32))
    amax = np.abs(blocks).max(-1, keepdims=True)
    byte = np.maximum(np.where(amax > 0, np.frexp(amax)[1] - 1 + 127, 0) - down, 1)
    scale = np.exp2(byte - 127.0)
    codes = (blocks / scale).astype(np.float32).astype(dtype).astype(np.float64)
    return np.moveaxis((codes * scale).reshape(v.shape), -1, axis)


WIDE = False


def mx_kscale(k):
    if not WIDE:
        return np.ones(k)
    levels = np.array([10, -10, 5, -5, 0])
    if k % 512:
        return np.exp2(np.random.permutation(np.resize(levels, k // 32))).repeat(32)
    a = np.empty((k // 512, 16))
    for p in range(k // 512):
        a[p, :8] = np.random.permutation(np.resize(levels, 8))
        for g in range(8):
            far = levels[np.abs(levels - a[p, g]) >= 10]
            a[p, g + 8] = far[np.random.randint(len(far))]
    return np.exp2(a.ravel()).repeat(32)


BF16 = ml_dtypes.bfloat16


def bf(x):
    return np.asarray(x, np.float32).astype(BF16)


def f64(x):
    return np.asarray(x).astype(np.float64)


E2M1 = np.array([0.0, 0.5, 1.0, 1.5, 2.0, 3.0, 4.0, 6.0, -0.0, -0.5, -1.0, -1.5, -2.0, -3.0, -4.0, -6.0])


def pack_weight(w, fmt):
    k, n = w.shape
    w = f64(bf(w)).reshape(k // 32, 32, n)
    amax = np.abs(w).max(1)
    if fmt == "e4m3":
        byte = np.frexp(amax)[1] - 1 + 127 - 7
    else:
        mant, ex = np.frexp(amax / 6.0)
        byte = np.where(mant > 0.5, ex, ex - 1) + 127
    byte = np.clip(np.where(amax > 0, byte, 1), 1, 254)
    scaled = (w * np.exp2(127.0 - byte)[:, None, :]).reshape(k, n).astype(np.float32)
    by_word = np.ascontiguousarray(scaled.reshape(k // 512, 128, 4, n).transpose(0, 1, 3, 2))
    if fmt == "e4m3":
        words = by_word.astype(ml_dtypes.float8_e4m3fn).view(np.uint8)
    else:
        c = by_word.astype(ml_dtypes.float4_e2m1fn).view(np.uint8) & 0xF
        words = c[..., 0::2] | (c[..., 1::2] << 4)
    return np.ascontiguousarray(words), np.ascontiguousarray(byte.astype(np.uint8).reshape(k // 512, 16, n))


def unpack_weight(words, scales, fmt):
    g, p, n, _ = words.shape
    if fmt == "e4m3":
        vals = np.ascontiguousarray(words).view(ml_dtypes.float8_e4m3fn).astype(np.float64)
    else:
        nib = np.empty((g, p, n, 4), np.uint8)
        nib[..., 0::2] = words & 0xF
        nib[..., 1::2] = words >> 4
        vals = E2M1[nib]
    vals = vals * np.repeat(np.exp2(scales.astype(np.float64) - 127.0), 8, axis=1)[..., None]
    return vals.transpose(0, 1, 3, 2).reshape(g * 512, n)


B, S, H, NH, LAT = 4, 2048, 512, 4, 512
HD = H // NH
HALF = H // 2
R = HALF // 2
ROPE_BASE = 10000.0


def rope_table():
    inv_freq = 1.0 / ROPE_BASE ** (np.arange(0, R, 2) / R)
    freqs = np.outer(np.arange(S), inv_freq)
    emb = np.concatenate([freqs, freqs], -1)
    return np.cos(emb), np.sin(emb)


def apply_rotary(x, cos, sin):
    h = x.shape[-1] // 2
    x1, x2 = x[..., :h], x[..., h:]
    return np.concatenate([x1 * cos - x2 * sin, x1 * sin + x2 * cos], -1)


def draw0():
    s, t = mx_kscale(H), mx_kscale(LAT)
    cos, sin = rope_table()
    hidden_states = bf(np.random.standard_normal((B, S, H)) * s)
    Wq_down = np.random.standard_normal((LAT, H)) / np.sqrt(H) * t[:, None] / s
    Wq_down_words, Wq_down_scales = pack_weight(Wq_down.T, "e4m3")
    bq_down = bf(np.random.standard_normal(LAT) * 0.2 * t)
    Wq_up = np.random.standard_normal((HALF, LAT)) * 1.2 / np.sqrt(LAT) / t
    Wq_up_words, Wq_up_scales = pack_weight(Wq_up.T, "e4m3")
    return {"hidden_states": hidden_states,
            "Wq_down_words": Wq_down_words,
            "Wq_down_scales": Wq_down_scales,
            "bq_down": bq_down,
            "Wq_up_words": Wq_up_words,
            "Wq_up_scales": Wq_up_scales,
            "bq_up": bf(np.random.standard_normal(HALF) * 0.2),
            "rope_cos": bf(cos),
            "rope_sin": bf(sin)}


def core(hidden_states, Wq_down_words, Wq_down_scales, bq_down, Wq_up_words, Wq_up_scales, bq_up, rope_cos, rope_sin):
    q_lat = (mxq(f64(hidden_states), 2, "e4m3") @ unpack_weight(Wq_down_words, Wq_down_scales, "e4m3")) + f64(bq_down)
    q_half = (mxq(q_lat, 2, "e4m3") @ unpack_weight(Wq_up_words, Wq_up_scales, "e4m3")) + f64(bq_up)
    q = np.concatenate([q_half, apply_rotary(q_half, f64(rope_cos), f64(rope_sin))], -1)
    return q.reshape(B, S, NH, HD).transpose(0, 2, 1, 3)


def e4m3fn_bytes(y):
    return np.clip(np.asarray(y, np.float64), -448.0, 448.0).astype(np.float32).astype(ml_dtypes.float8_e4m3fn).view(np.uint8)


def e4m3fn_values(b):
    return np.asarray(b, np.uint8).view(ml_dtypes.float8_e4m3fn).astype(np.float64)


def setup_inputs():
    d = draw0()
    x0 = np.asarray(d['hidden_states']).astype(np.float64)
    s = (np.max(np.abs(x0), axis=(0, 1), keepdims=True) / 448.0).astype(np.float32)
    out = {}
    for k, v in d.items():
        if k == 'hidden_states':
            out['hidden_states_bytes'] = e4m3fn_bytes(x0 / s.astype(np.float64))
            out['hidden_states_scale'] = s
        else:
            out[k] = v
    return out


def reference(hidden_states_bytes, hidden_states_scale, Wq_down_words, Wq_down_scales, bq_down, Wq_up_words, Wq_up_scales, bq_up, rope_cos, rope_sin):
    return core(e4m3fn_values(hidden_states_bytes) * hidden_states_scale.astype(np.float64), Wq_down_words, Wq_down_scales, bq_down, Wq_up_words, Wq_up_scales, bq_up, rope_cos, rope_sin)

@@ -1,0 +1,268 @@
+from contextlib import ExitStack
+
+import concourse.mybir as mybir
+from concourse.masks import make_identity
+
+B, S, H, LAT, UP = 4, 2048, 512, 512, 256
+FLOPS = 2 * B * S * LAT * (H + UP)
+
+F32 = mybir.dt.float32
+BF16 = mybir.dt.bfloat16
+I32 = mybir.dt.int32
+U32 = mybir.dt.uint32
+U8 = mybir.dt.uint8
+FP8 = mybir.dt.float8_e4m3fn
+FP8X4 = mybir.dt.float8_e4m3fn_x4
+ACT = mybir.ActivationFunctionType
+ALU = mybir.AluOpType
+
+P = 128
+ROWS = S // P
+TILES = 2
+TOK = TILES * P
+PER_BATCH = ROWS // TILES
+UNITS = B * PER_BATCH
+STORE = 2
+XT, M1, M2, OT = 2, 2, 1, 3
+
+
+def tile_multiheadlatentattention_pa_t_w8_kernel(
+    tc, x_bytes, x_scale, wd_words, wd_scales, b_down, wu_words, wu_scales, b_up, rope_cos, rope_sin, out
+):
+    nc = tc.nc
+    with ExitStack() as ctx:
+        keep = ctx.enter_context(tc.tile_pool(name="keep", bufs=1))
+        work = ctx.enter_context(tc.tile_pool(name="work", bufs=3))
+        psum = ctx.enter_context(tc.psum_pool(name="psum", bufs=2))
+        ctx.enter_context(tc.manual_schedule())
+
+        wsc_raw = keep.tile([P, LAT + UP], U8, align_bytes=64)
+        nc.vector.memset(wsc_raw[:].bitcast(I32), 0)
+        ident = keep.tile([P, P], F32)
+        make_identity(nc, ident[:])
+        ident_b = keep.tile([P, P], BF16)
+        nc.vector.tensor_copy(out=ident_b[:], in_=ident[:])
+
+
+        pieces = {}
+
+        def load_x(b, i0, n):
+            xb8 = keep.tile([P, n * H], U8, name="x8_%d_%d" % (b, i0), align_bytes=64)
+            src = x_bytes[b].rearrange("(p i) k -> p i k", i=ROWS)[:, i0 : i0 + n, :]
+            nc.sync.dma_start(out=xb8[:].rearrange("p (i k) -> p i k", k=H), in_=src)
+            for i in range(n):
+                pieces[(b, i0 + i)] = (xb8, i)
+
+        load_x(0, 0, 2)
+        sc = keep.tile([P, 4], F32)
+        nc.sync.dma_start(out=sc[:], in_=x_scale.rearrange("a o (p t) -> p (a o t)", t=4))
+        wd_raw = keep.tile([P, LAT], U32)
+        nc.sync.dma_start(out=wd_raw[:].bitcast(I32), in_=wd_words[0].rearrange("p n t -> p (n t)").bitcast(I32))
+        for r in range(4):
+            nc.sync.dma_start(
+                out=wsc_raw[r : P : 32, 0:LAT].bitcast(I32),
+                in_=wd_scales[0].rearrange("(q r) n -> r q n", r=4)[r].bitcast(I32),
+            )
+        bd_b = keep.tile([P, 4], BF16)
+        nc.sync.dma_start(out=bd_b[:], in_=b_down.rearrange("(p t) -> p t", t=4))
+        load_x(0, 2, 2)
+        rope_c = keep.tile([P, ROWS, P], BF16)
+        nc.sync.dma_start(out=rope_c[:], in_=rope_cos.rearrange("(p i) d -> p i d", i=ROWS))
+        rope_s = keep.tile([P, ROWS, P], BF16)
+        nc.sync.dma_start(out=rope_s[:], in_=rope_sin.rearrange("(p i) d -> p i d", i=ROWS))
+        wu = keep.tile([P, UP], U32, align_bytes=64)
+        nc.sync.dma_start(out=wu[:].bitcast(I32), in_=wu_words[0].rearrange("p n t -> p (n t)").bitcast(I32))
+        for r in range(4):
+            nc.sync.dma_start(
+                out=wsc_raw[r : P : 32, LAT : LAT + UP].bitcast(I32),
+                in_=wu_scales[0].rearrange("(q r) n -> r q n", r=4)[r].bitcast(I32),
+            )
+        bu_b = keep.tile([P, 2], BF16)
+        with nc.allow_non_contiguous_dma(reason="256 bias values, once"):
+            nc.sync.dma_start(out=bu_b[:], in_=b_up.rearrange("(h p) -> p h", p=P))
+        load_x(0, 4, 4)
+        load_x(0, 8, 8)
+        for b in range(1, B):
+            load_x(b, 0, 8)
+            load_x(b, 8, 8)
+
+        wd = keep.tile([P, LAT], U32, align_bytes=64)
+        wdsc = keep.tile([P, LAT], U8, align_bytes=64)
+        bd = keep.tile([P, 4], F32)
+        bu = keep.tile([P, 2], F32)
+        tabs = keep.tile([P, 3, S], BF16)
+
+        D = 2
+        xs, m1, pairs, codes, planes_, m2, xbias, pv, pg, outs, obank, xbank = ({} for i in range(12))
+
+        def pair(n):
+            if n not in pairs:
+                both = work.tile([P, 2 * TOK * 4], BF16, align_bytes=64, name="pair", bufs=4)
+                pairs[n] = both
+            return pairs[n]
+
+        def cast(u):
+            b, i0 = u // PER_BATCH, TILES * (u % PER_BATCH)
+            tile8, i = pieces[(b, i0)]
+            plain = work.tile([P, TILES * H], BF16, align_bytes=64, bufs=4)
+            nc.scalar.copy(out=plain[:], in_=tile8[:, i * H : (i + TILES) * H].bitcast(FP8))
+            xs[u] = plain
+
+        def turn_x(u):
+            words = xs[u][:].bitcast(F32)
+            bank = psum.tile([P, 2, TOK], F32, name="xt", bufs=XT)
+            for j in range(TILES):
+                for w in range(2):
+                    nc.tensor.transpose(bank[:, w, j * P : (j + 1) * P], words[:, j * 256 + w : (j + 1) * 256 : 2], ident[:])
+            xbank[u] = bank
+
+        def scale_x(u):
+            nc.vector.tensor_tensor(
+                out=pair(u)[:, 0 : TOK * 4].rearrange("p (r w e) -> p r w e", w=2, e=2),
+                in0=xbank[u][:].rearrange("p w r -> p (w r)").bitcast(BF16).rearrange("p (w r e) -> p r w e", w=2, e=2),
+                in1=sc[:].rearrange("p (w e) -> p w e", e=2).unsqueeze(1).to_broadcast([P, TOK, 2, 2]),
+                op=ALU.mult,
+            )
+
+        def quant(n):
+            lo = 0 if n < UNITS else TOK
+            hi = 2 * TOK if n >= D else TOK
+            words = work.tile([P, 2 * TOK], U32, align_bytes=64, bufs=4)
+            plane = work.tile([P, 2 * TOK], U8, align_bytes=64, bufs=4)
+            nc.vector.quantize_mx(
+                out=words[:, lo:hi].bitcast(FP8X4), scales=plane[:, lo:hi], in_=pairs[n][:, 4 * lo : 4 * hi]
+            )
+            codes[n], planes_[n] = words, plane
+
+        def down(u, j):
+            bank = psum.tile([P, 4, P], F32, name="m1", bufs=M1)
+            for t in range(4):
+                nc.tensor.matmul_mx(
+                    out=bank[:, t, :],
+                    lhsT=wd[:, t * P : (t + 1) * P].bitcast(FP8X4),
+                    lhsT_scale=wdsc[:, t * P : (t + 1) * P],
+                    rhs=codes[u][:, j * P : (j + 1) * P].bitcast(FP8X4),
+                    rhs_scale=planes_[u][:, j * P : (j + 1) * P],
+                    start=True,
+                    stop=True,
+                )
+            m1[u, j] = bank
+
+        def leave_down(u, j):
+            nc.vector.tensor_tensor(
+                out=pair(u + D)[:, (TILES + j) * 512 : (TILES + j + 1) * 512].rearrange("p (r t) -> p r t", t=4),
+                in0=m1[u, j][:].rearrange("p t r -> p r t"),
+                in1=bd[:].unsqueeze(1).to_broadcast([P, P, 4]),
+                op=ALU.add,
+            )
+
+        def up(u):
+            bank = psum.tile([P, 2, TOK], F32, name="m2", bufs=M2)
+            for h in (1, 0):
+                nc.tensor.matmul_mx(
+                    out=bank[:, h, :],
+                    lhsT=wu[:, h * P : (h + 1) * P].bitcast(FP8X4),
+                    lhsT_scale=wsc_raw[:, LAT + h * P : LAT + (h + 1) * P],
+                    rhs=codes[u + D][:, TOK : 2 * TOK].bitcast(FP8X4),
+                    rhs_scale=planes_[u + D][:, TOK : 2 * TOK],
+                    start=True,
+                    stop=True,
+                )
+            m2[u] = bank
+
+        def bias_up(u):
+            biased = work.tile([P, 2, TOK], F32, bufs=4)
+            for h in (1, 0):
+                nc.scalar.activation(
+                    out=biased[:, h, :], in_=m2[u][:, h, :], func=ACT.Identity, bias=bu[:, h : h + 1]
+                )
+            xbias[u] = biased
+
+        def products(u, h, engine):
+            c0 = (u % PER_BATCH) * TOK
+            prod = work.tile([P, 2, TOK], F32, name="prod%d" % h, bufs=4)
+            engine.tensor_tensor(
+                out=prod[:],
+                in0=xbias[u][:, h, :].unsqueeze(1).to_broadcast([P, 2, TOK]),
+                in1=tabs[:, 1 - h : 3 - h, c0 : c0 + TOK],
+                op=ALU.mult,
+            )
+            (pg if h else pv)[u] = prod
+
+        def turn_out(u, j):
+            cols = slice(j * P, (j + 1) * P)
+            bank = psum.tile([P, 4, P], F32, name="ot", bufs=OT)
+            for h in range(2):
+                nc.tensor.transpose(bank[:, h, :], xbias[u][:, h, cols], ident[:])
+            for h in range(2):
+                nc.tensor.matmul(
+                    bank[:, 2 + h, :], pg[u][:, h, cols], ident[:], start=True, stop=False, is_transpose=True
+                )
+                nc.tensor.matmul(
+                    bank[:, 2 + h, :], pv[u][:, h, cols], ident[:], start=False, stop=True, is_transpose=True
+                )
+            obank[u, j] = bank
+
+        def leave_out(u, j):
+            n = u // STORE
+            if n not in outs:
+                stage = work.tile([P, 4, STORE * TILES, P], F32, name="stage", bufs=3)
+                outs[n] = stage
+            nc.scalar.copy(out=outs[n][:, :, (u % STORE) * TILES + j, :], in_=obank[u, j][:])
+            if j == TILES - 1 and u % STORE == STORE - 1:
+                b, i0 = n * STORE // PER_BATCH, TILES * (n * STORE % PER_BATCH)
+                dst = out[b].rearrange("h (p i) d -> p h i d", i=ROWS)[:, :, i0 : i0 + STORE * TILES, :]
+                nc.sync.dma_start(
+                    out=dst.rearrange("p h i d -> p h (i d)"), in_=outs[n][:].rearrange("p h i d -> p h (i d)")
+                )
+
+        def tables(u):
+            if u >= PER_BATCH:
+                return
+            bank = psum.tile([P, 2, TILES, P], BF16, name="ot", bufs=OT)
+            for j in range(TILES):
+                nc.tensor.transpose(bank[:, 0, j, :], rope_c[:, u * TILES + j, :], ident_b[:])
+                nc.tensor.transpose(bank[:, 1, j, :], rope_s[:, u * TILES + j, :], ident_b[:])
+            cols = slice(u * TOK, (u + 1) * TOK)
+            nc.scalar.copy(out=tabs[:, 1:3, cols], in_=bank[:].rearrange("p a j r -> p a (j r)"))
+            nc.scalar.activation(
+                out=tabs[:, 0, cols], in_=bank[:, 1].rearrange("p j r -> p (j r)"), func=ACT.Copy, scale=-1.0
+            )
+
+        def g_products(u, h):
+            last = u == UNITS - 1 and h == 0
+            products(u, h, nc.vector if last else nc.gpsimd)
+
+        nc.vector.tensor_copy(
+            out=wd[:].bitcast(I32).rearrange("p (t m) -> p t m", t=4),
+            in_=wd_raw[:].bitcast(I32).rearrange("p (m t) -> p t m", t=4),
+        )
+        nc.vector.tensor_copy(
+            out=wdsc[:].rearrange("p (t m) -> p m t", t=4), in_=wsc_raw[:, 0:LAT].rearrange("p (m t) -> p m t", t=4)
+        )
+        nc.vector.tensor_copy(out=bd[:], in_=bd_b[:])
+        nc.vector.tensor_copy(out=bu[:], in_=bu_b[:])
+
+        order = [
+            (up, 8),
+            (cast, 0),
+            (lambda u: down(u, 0), 6),
+            (lambda u: leave_out(u, 1), 11),
+            (lambda u: g_products(u, 1), 10),
+            (lambda u: g_products(u, 0), 10),
+            (bias_up, 8),
+            (lambda u: turn_out(u, 0), 10),
+            (lambda u: leave_down(u, 0), 6),
+            (quant, 5),
+            (turn_x, 3),
+            (lambda u: leave_out(u, 0), 10),
+            (lambda u: turn_out(u, 1), 10),
+            (scale_x, 4),
+            (lambda u: down(u, 1), 6),
+            (lambda u: leave_down(u, 1), 6),
+            (tables, 7),
+        ]
+        for s in range(UNITS + D + 12):
+            for stage, lag in order:
+                if 0 <= s - lag < UNITS + (D if stage is quant else 0):
+                    stage(s - lag)

@@ -23,7 +23,10 @@ TOK = TILES * P
 PER_BATCH = ROWS // TILES
 UNITS = B * PER_BATCH
 STORE = 2
-XT, M1, M2, OT = 2, 2, 1, 3
+DEPTH = 8
+BANKS = 8
+MU = 2
+TAIL = 2
 
 
 def tile_multiheadlatentattention_pa_t_w8_kernel(
@@ -92,25 +95,25 @@ def tile_multiheadlatentattention_pa_t_w8_kernel(
         bu = keep.tile([P, 2], F32)
         tabs = keep.tile([P, 3, S], BF16)
 
-        D = 2
-        xs, m1, pairs, codes, planes_, m2, xbias, pv, pg, outs, obank, xbank = ({} for i in range(12))
+        D = 4
+        xs, m1, pairs, codes, planes_, m2, xbias, prods, outs, obank, xbank, left = ({} for i in range(12))
 
         def pair(n):
             if n not in pairs:
-                both = work.tile([P, 2 * TOK * 4], BF16, align_bytes=64, name="pair", bufs=4)
+                both = work.tile([P, 2 * TOK * 4], BF16, align_bytes=64, name="pair", bufs=DEPTH)
                 pairs[n] = both
             return pairs[n]
 
         def cast(u):
             b, i0 = u // PER_BATCH, TILES * (u % PER_BATCH)
             tile8, i = pieces[(b, i0)]
-            plain = work.tile([P, TILES * H], BF16, align_bytes=64, bufs=4)
+            plain = work.tile([P, TILES * H], BF16, align_bytes=64, bufs=DEPTH)
             nc.scalar.copy(out=plain[:], in_=tile8[:, i * H : (i + TILES) * H].bitcast(FP8))
             xs[u] = plain
 
         def turn_x(u):
             words = xs[u][:].bitcast(F32)
-            bank = psum.tile([P, 2, TOK], F32, name="xt", bufs=XT)
+            bank = psum.tile([P, 2, TOK], F32, name="bank", bufs=BANKS)
             for j in range(TILES):
                 for w in range(2):
                     nc.tensor.transpose(bank[:, w, j * P : (j + 1) * P], words[:, j * 256 + w : (j + 1) * 256 : 2], ident[:])
@@ -127,15 +130,15 @@ def tile_multiheadlatentattention_pa_t_w8_kernel(
         def quant(n):
             lo = 0 if n < UNITS else TOK
             hi = 2 * TOK if n >= D else TOK
-            words = work.tile([P, 2 * TOK], U32, align_bytes=64, bufs=4)
-            plane = work.tile([P, 2 * TOK], U8, align_bytes=64, bufs=4)
+            words = work.tile([P, 2 * TOK], U32, align_bytes=64, bufs=DEPTH)
+            plane = work.tile([P, 2 * TOK], U8, align_bytes=64, bufs=DEPTH)
             nc.vector.quantize_mx(
                 out=words[:, lo:hi].bitcast(FP8X4), scales=plane[:, lo:hi], in_=pairs[n][:, 4 * lo : 4 * hi]
             )
             codes[n], planes_[n] = words, plane
 
         def down(u, j):
-            bank = psum.tile([P, 4, P], F32, name="m1", bufs=M1)
+            bank = psum.tile([P, 4, P], F32, name="bank", bufs=BANKS)
             for t in range(4):
                 nc.tensor.matmul_mx(
                     out=bank[:, t, :],
@@ -157,7 +160,7 @@ def tile_multiheadlatentattention_pa_t_w8_kernel(
             )
 
         def up(u):
-            bank = psum.tile([P, 2, TOK], F32, name="m2", bufs=M2)
+            bank = psum.tile([P, 2, TOK], F32, name="bank", bufs=BANKS)
             for h in (1, 0):
                 nc.tensor.matmul_mx(
                     out=bank[:, h, :],
@@ -171,45 +174,73 @@ def tile_multiheadlatentattention_pa_t_w8_kernel(
             m2[u] = bank
 
         def bias_up(u):
-            biased = work.tile([P, 2, TOK], F32, bufs=4)
+            biased = work.tile([P, 2, TOK], F32, bufs=DEPTH)
             for h in (1, 0):
                 nc.scalar.activation(
                     out=biased[:, h, :], in_=m2[u][:, h, :], func=ACT.Identity, bias=bu[:, h : h + 1]
                 )
             xbias[u] = biased
 
-        def products(u, h, engine):
+        def on_vector(u, h):
+            return u >= UNITS - TAIL or (h == 0 and u % 4 == 1)
+
+        def prod(u, h):
+            if (u, h) not in prods:
+                pairs_of = work.tile([P, 2, TOK], F32, name="prod%d" % h, bufs=DEPTH)
+                prods[u, h] = pairs_of
+            return prods[u, h]
+
+        def mix(u):
             c0 = (u % PER_BATCH) * TOK
-            prod = work.tile([P, 2, TOK], F32, name="prod%d" % h, bufs=4)
-            engine.tensor_tensor(
-                out=prod[:],
-                in0=xbias[u][:, h, :].unsqueeze(1).to_broadcast([P, 2, TOK]),
-                in1=tabs[:, 1 - h : 3 - h, c0 : c0 + TOK],
-                op=ALU.mult,
-            )
-            (pg if h else pv)[u] = prod
+            for h in [h for h in (1, 0) if on_vector(u, h)]:
+                nc.vector.scalar_tensor_tensor(
+                    out=prod(u, h)[:],
+                    in0=m2[u][:, h, :].unsqueeze(1).to_broadcast([P, 2, TOK]),
+                    scalar=bu[:, h : h + 1],
+                    in1=tabs[:, 1 - h : 3 - h, c0 : c0 + TOK],
+                    op0=ALU.add,
+                    op1=ALU.mult,
+                )
+
+        def products(u):
+            c0 = (u % PER_BATCH) * TOK
+            for h in [h for h in (1, 0) if not on_vector(u, h)]:
+                nc.gpsimd.tensor_tensor(
+                    out=prod(u, h)[:],
+                    in0=xbias[u][:, h, :].unsqueeze(1).to_broadcast([P, 2, TOK]),
+                    in1=tabs[:, 1 - h : 3 - h, c0 : c0 + TOK],
+                    op=ALU.mult,
+                )
 
         def turn_out(u, j):
             cols = slice(j * P, (j + 1) * P)
-            bank = psum.tile([P, 4, P], F32, name="ot", bufs=OT)
+            bank = psum.tile([P, 4, P], F32, name="bank", bufs=BANKS)
             for h in range(2):
                 nc.tensor.transpose(bank[:, h, :], xbias[u][:, h, cols], ident[:])
             for h in range(2):
                 nc.tensor.matmul(
-                    bank[:, 2 + h, :], pg[u][:, h, cols], ident[:], start=True, stop=False, is_transpose=True
+                    bank[:, 2 + h, :], prods[u, 1][:, h, cols], ident[:], start=True, stop=False, is_transpose=True
                 )
                 nc.tensor.matmul(
-                    bank[:, 2 + h, :], pv[u][:, h, cols], ident[:], start=False, stop=True, is_transpose=True
+                    bank[:, 2 + h, :], prods[u, 0][:, h, cols], ident[:], start=False, stop=True, is_transpose=True
                 )
             obank[u, j] = bank
 
         def leave_out(u, j):
             n = u // STORE
+            if n == UNITS // STORE - 1:
+                one = work.tile([P, 4, P], F32, name="one", bufs=4)
+                copy = nc.vector.tensor_copy if (u == UNITS - 1 and j == 1) else nc.scalar.copy
+                copy(out=one[:], in_=obank[u, j][:])
+                b, i0 = u // PER_BATCH, TILES * (u % PER_BATCH) + j
+                nc.sync.dma_start(out=out[b].rearrange("h (p i) d -> p h i d", i=ROWS)[:, :, i0, :], in_=one[:])
+                return
+            left[n] = left.get(n, STORE * TILES) - 1
             if n not in outs:
                 stage = work.tile([P, 4, STORE * TILES, P], F32, name="stage", bufs=3)
                 outs[n] = stage
             nc.scalar.copy(out=outs[n][:, :, (u % STORE) * TILES + j, :], in_=obank[u, j][:])
-            if j == TILES - 1 and u % STORE == STORE - 1:
+            if left[n] == 0:
                 b, i0 = n * STORE // PER_BATCH, TILES * (n * STORE % PER_BATCH)
                 dst = out[b].rearrange("h (p i) d -> p h i d", i=ROWS)[:, :, i0 : i0 + STORE * TILES, :]
                 nc.sync.dma_start(
@@ -219,7 +250,7 @@ def tile_multiheadlatentattention_pa_t_w8_kernel(
         def tables(u):
             if u >= PER_BATCH:
                 return
-            bank = psum.tile([P, 2, TILES, P], BF16, name="ot", bufs=OT)
+            bank = psum.tile([P, 2, TILES, P], BF16, name="bank", bufs=BANKS)
             for j in range(TILES):
                 nc.tensor.transpose(bank[:, 0, j, :], rope_c[:, u * TILES + j, :], ident_b[:])
                 nc.tensor.transpose(bank[:, 1, j, :], rope_s[:, u * TILES + j, :], ident_b[:])
@@ -228,10 +259,6 @@ def tile_multiheadlatentattention_pa_t_w8_kernel(
             nc.scalar.activation(
                 out=tabs[:, 0, cols], in_=bank[:, 1].rearrange("p j r -> p (j r)"), func=ACT.Copy, scale=-1.0
             )
-
-        def g_products(u, h):
-            last = u == UNITS - 1 and h == 0
-            products(u, h, nc.vector if last else nc.gpsimd)
 
         nc.vector.tensor_copy(
             out=wd[:].bitcast(I32).rearrange("p (t m) -> p t m", t=4),
@@ -244,25 +271,43 @@ def tile_multiheadlatentattention_pa_t_w8_kernel(
         nc.vector.tensor_copy(out=bu[:], in_=bu_b[:])
 
         order = [
-            (up, 8),
-            (cast, 0),
-            (lambda u: down(u, 0), 6),
-            (lambda u: leave_out(u, 1), 11),
-            (lambda u: g_products(u, 1), 10),
-            (lambda u: g_products(u, 0), 10),
-            (bias_up, 8),
-            (lambda u: turn_out(u, 0), 10),
-            (lambda u: leave_down(u, 0), 6),
-            (quant, 5),
-            (turn_x, 3),
-            (lambda u: leave_out(u, 0), 10),
-            (lambda u: turn_out(u, 1), 10),
-            (scale_x, 4),
-            (lambda u: down(u, 1), 6),
-            (lambda u: leave_down(u, 1), 6),
-            (tables, 7),
+            (lambda u: leave_out(u, 1), 1, 7),
+            (turn_x, 1, 2),
+            (products, 1, 6),
+            (lambda u: leave_out(u, 0), 0, 6),
+            (lambda u: leave_down(u, 0), 1, 5),
+            (lambda u: leave_down(u, 0), 0, 4),
+            (lambda u: leave_out(u, 1), 0, 6),
+            (tables, 0, 3),
+            (tables, 1, 3),
+            (turn_x, 0, 1),
+            (cast, 1, 1),
+            (lambda u: down(u, 0), 0, 3),
+            (quant, 1, 3),
+            (up, 1, 5),
+            (lambda u: down(u, 1), 0, 3),
+            (products, 0, 5),
+            (quant, 0, 2),
+            (scale_x, 1, 2),
+            (up, 0, 4),
+            (bias_up, 1, 5),
+            (lambda u: down(u, 1), 1, 3),
+            (lambda u: leave_down(u, 1), 0, 3),
+            (lambda u: leave_down(u, 1), 1, 4),
+            (bias_up, 0, 4),
+            (mix, 0, 5),
+            (cast, 0, 0),
+            (lambda u: down(u, 0), 1, 4),
+            (lambda u: turn_out(u, 0), 1, 6),
+            (scale_x, 0, 1),
+            (lambda u: turn_out(u, 1), 1, 6),
+            (mix, 1, 5),
+            (lambda u: turn_out(u, 0), 0, 5),
+            (lambda u: turn_out(u, 1), 0, 5),
+            (lambda u: leave_out(u, 0), 1, 6),
         ]
-        for s in range(UNITS + D + 12):
-            for stage, lag in order:
-                if 0 <= s - lag < UNITS + (D if stage is quant else 0):
-                    stage(s - lag)
+        for s in range((UNITS + D) // MU + 7 + 1):
+            for stage, r, lag in order:
+                u = MU * (s - lag) + r
+                if 0 <= u < UNITS + (D if stage is quant else 0):
+                    stage(u)

from contextlib import ExitStack

import concourse.mybir as mybir
from concourse.masks import make_identity

B, S, H, LAT, UP = 4, 2048, 512, 512, 256
FLOPS = 2 * B * S * LAT * (H + UP)

F32 = mybir.dt.float32
BF16 = mybir.dt.bfloat16
I32 = mybir.dt.int32
U32 = mybir.dt.uint32
U8 = mybir.dt.uint8
FP8 = mybir.dt.float8_e4m3fn
FP8X4 = mybir.dt.float8_e4m3fn_x4
ACT = mybir.ActivationFunctionType
ALU = mybir.AluOpType

P = 128
ROWS = S // P
TILES = 2
TOK = TILES * P
PER_BATCH = ROWS // TILES
UNITS = B * PER_BATCH
STORE = 2
DEPTH = 8
BANKS = 8
MU = 2
TAIL = 2


def tile_multiheadlatentattention_pa_t_w8_kernel(
    tc, x_bytes, x_scale, wd_words, wd_scales, b_down, wu_words, wu_scales, b_up, rope_cos, rope_sin, out
):
    nc = tc.nc
    with ExitStack() as ctx:
        keep = ctx.enter_context(tc.tile_pool(name="keep", bufs=1))
        work = ctx.enter_context(tc.tile_pool(name="work", bufs=3))
        psum = ctx.enter_context(tc.psum_pool(name="psum", bufs=2))
        ctx.enter_context(tc.manual_schedule())

        wsc_raw = keep.tile([P, LAT + UP], U8, align_bytes=64)
        nc.vector.memset(wsc_raw[:].bitcast(I32), 0)
        ident = keep.tile([P, P], F32)
        make_identity(nc, ident[:])
        ident_b = keep.tile([P, P], BF16)
        nc.vector.tensor_copy(out=ident_b[:], in_=ident[:])


        pieces = {}

        def load_x(b, i0, n):
            xb8 = keep.tile([P, n * H], U8, name="x8_%d_%d" % (b, i0), align_bytes=64)
            src = x_bytes[b].rearrange("(p i) k -> p i k", i=ROWS)[:, i0 : i0 + n, :]
            nc.sync.dma_start(out=xb8[:].rearrange("p (i k) -> p i k", k=H), in_=src)
            for i in range(n):
                pieces[(b, i0 + i)] = (xb8, i)

        load_x(0, 0, 2)
        sc = keep.tile([P, 4], F32)
        nc.sync.dma_start(out=sc[:], in_=x_scale.rearrange("a o (p t) -> p (a o t)", t=4))
        wd_raw = keep.tile([P, LAT], U32)
        nc.sync.dma_start(out=wd_raw[:].bitcast(I32), in_=wd_words[0].rearrange("p n t -> p (n t)").bitcast(I32))
        for r in range(4):
            nc.sync.dma_start(
                out=wsc_raw[r : P : 32, 0:LAT].bitcast(I32),
                in_=wd_scales[0].rearrange("(q r) n -> r q n", r=4)[r].bitcast(I32),
            )
        bd_b = keep.tile([P, 4], BF16)
        nc.sync.dma_start(out=bd_b[:], in_=b_down.rearrange("(p t) -> p t", t=4))
        load_x(0, 2, 2)
        rope_c = keep.tile([P, ROWS, P], BF16)
        nc.sync.dma_start(out=rope_c[:], in_=rope_cos.rearrange("(p i) d -> p i d", i=ROWS))
        rope_s = keep.tile([P, ROWS, P], BF16)
        nc.sync.dma_start(out=rope_s[:], in_=rope_sin.rearrange("(p i) d -> p i d", i=ROWS))
        wu = keep.tile([P, UP], U32, align_bytes=64)
        nc.sync.dma_start(out=wu[:].bitcast(I32), in_=wu_words[0].rearrange("p n t -> p (n t)").bitcast(I32))
        for r in range(4):
            nc.sync.dma_start(
                out=wsc_raw[r : P : 32, LAT : LAT + UP].bitcast(I32),
                in_=wu_scales[0].rearrange("(q r) n -> r q n", r=4)[r].bitcast(I32),
            )
        bu_b = keep.tile([P, 2], BF16)
        with nc.allow_non_contiguous_dma(reason="256 bias values, once"):
            nc.sync.dma_start(out=bu_b[:], in_=b_up.rearrange("(h p) -> p h", p=P))
        load_x(0, 4, 4)
        load_x(0, 8, 8)
        for b in range(1, B):
            load_x(b, 0, 8)
            load_x(b, 8, 8)

        wd = keep.tile([P, LAT], U32, align_bytes=64)
        wdsc = keep.tile([P, LAT], U8, align_bytes=64)
        bd = keep.tile([P, 4], F32)
        bu = keep.tile([P, 2], F32)
        tabs = keep.tile([P, 3, S], BF16)

        D = 4
        xs, m1, pairs, codes, planes_, m2, xbias, prods, outs, obank, xbank, left = ({} for i in range(12))

        def pair(n):
            if n not in pairs:
                both = work.tile([P, 2 * TOK * 4], BF16, align_bytes=64, name="pair", bufs=DEPTH)
                pairs[n] = both
            return pairs[n]

        def cast(u):
            b, i0 = u // PER_BATCH, TILES * (u % PER_BATCH)
            tile8, i = pieces[(b, i0)]
            plain = work.tile([P, TILES * H], BF16, align_bytes=64, bufs=DEPTH)
            nc.scalar.copy(out=plain[:], in_=tile8[:, i * H : (i + TILES) * H].bitcast(FP8))
            xs[u] = plain

        def turn_x(u):
            words = xs[u][:].bitcast(F32)
            bank = psum.tile([P, 2, TOK], F32, name="bank", bufs=BANKS)
            for j in range(TILES):
                for w in range(2):
                    nc.tensor.transpose(bank[:, w, j * P : (j + 1) * P], words[:, j * 256 + w : (j + 1) * 256 : 2], ident[:])
            xbank[u] = bank

        def scale_x(u):
            nc.vector.tensor_tensor(
                out=pair(u)[:, 0 : TOK * 4].rearrange("p (r w e) -> p r w e", w=2, e=2),
                in0=xbank[u][:].rearrange("p w r -> p (w r)").bitcast(BF16).rearrange("p (w r e) -> p r w e", w=2, e=2),
                in1=sc[:].rearrange("p (w e) -> p w e", e=2).unsqueeze(1).to_broadcast([P, TOK, 2, 2]),
                op=ALU.mult,
            )

        def quant(n):
            lo = 0 if n < UNITS else TOK
            hi = 2 * TOK if n >= D else TOK
            words = work.tile([P, 2 * TOK], U32, align_bytes=64, bufs=DEPTH)
            plane = work.tile([P, 2 * TOK], U8, align_bytes=64, bufs=DEPTH)
            nc.vector.quantize_mx(
                out=words[:, lo:hi].bitcast(FP8X4), scales=plane[:, lo:hi], in_=pairs[n][:, 4 * lo : 4 * hi]
            )
            codes[n], planes_[n] = words, plane

        def down(u, j):
            bank = psum.tile([P, 4, P], F32, name="bank", bufs=BANKS)
            for t in range(4):
                nc.tensor.matmul_mx(
                    out=bank[:, t, :],
                    lhsT=wd[:, t * P : (t + 1) * P].bitcast(FP8X4),
                    lhsT_scale=wdsc[:, t * P : (t + 1) * P],
                    rhs=codes[u][:, j * P : (j + 1) * P].bitcast(FP8X4),
                    rhs_scale=planes_[u][:, j * P : (j + 1) * P],
                    start=True,
                    stop=True,
                )
            m1[u, j] = bank

        def leave_down(u, j):
            nc.vector.tensor_tensor(
                out=pair(u + D)[:, (TILES + j) * 512 : (TILES + j + 1) * 512].rearrange("p (r t) -> p r t", t=4),
                in0=m1[u, j][:].rearrange("p t r -> p r t"),
                in1=bd[:].unsqueeze(1).to_broadcast([P, P, 4]),
                op=ALU.add,
            )

        def up(u):
            bank = psum.tile([P, 2, TOK], F32, name="bank", bufs=BANKS)
            for h in (1, 0):
                nc.tensor.matmul_mx(
                    out=bank[:, h, :],
                    lhsT=wu[:, h * P : (h + 1) * P].bitcast(FP8X4),
                    lhsT_scale=wsc_raw[:, LAT + h * P : LAT + (h + 1) * P],
                    rhs=codes[u + D][:, TOK : 2 * TOK].bitcast(FP8X4),
                    rhs_scale=planes_[u + D][:, TOK : 2 * TOK],
                    start=True,
                    stop=True,
                )
            m2[u] = bank

        def bias_up(u):
            biased = work.tile([P, 2, TOK], F32, bufs=DEPTH)
            for h in (1, 0):
                nc.scalar.activation(
                    out=biased[:, h, :], in_=m2[u][:, h, :], func=ACT.Identity, bias=bu[:, h : h + 1]
                )
            xbias[u] = biased

        def on_vector(u, h):
            return u >= UNITS - TAIL or (h == 0 and u % 4 == 1)

        def prod(u, h):
            if (u, h) not in prods:
                pairs_of = work.tile([P, 2, TOK], F32, name="prod%d" % h, bufs=DEPTH)
                prods[u, h] = pairs_of
            return prods[u, h]

        def mix(u):
            c0 = (u % PER_BATCH) * TOK
            for h in [h for h in (1, 0) if on_vector(u, h)]:
                nc.vector.scalar_tensor_tensor(
                    out=prod(u, h)[:],
                    in0=m2[u][:, h, :].unsqueeze(1).to_broadcast([P, 2, TOK]),
                    scalar=bu[:, h : h + 1],
                    in1=tabs[:, 1 - h : 3 - h, c0 : c0 + TOK],
                    op0=ALU.add,
                    op1=ALU.mult,
                )

        def products(u):
            c0 = (u % PER_BATCH) * TOK
            for h in [h for h in (1, 0) if not on_vector(u, h)]:
                nc.gpsimd.tensor_tensor(
                    out=prod(u, h)[:],
                    in0=xbias[u][:, h, :].unsqueeze(1).to_broadcast([P, 2, TOK]),
                    in1=tabs[:, 1 - h : 3 - h, c0 : c0 + TOK],
                    op=ALU.mult,
                )

        def turn_out(u, j):
            cols = slice(j * P, (j + 1) * P)
            bank = psum.tile([P, 4, P], F32, name="bank", bufs=BANKS)
            for h in range(2):
                nc.tensor.transpose(bank[:, h, :], xbias[u][:, h, cols], ident[:])
            for h in range(2):
                nc.tensor.matmul(
                    bank[:, 2 + h, :], prods[u, 1][:, h, cols], ident[:], start=True, stop=False, is_transpose=True
                )
                nc.tensor.matmul(
                    bank[:, 2 + h, :], prods[u, 0][:, h, cols], ident[:], start=False, stop=True, is_transpose=True
                )
            obank[u, j] = bank

        def leave_out(u, j):
            n = u // STORE
            if n == UNITS // STORE - 1:
                one = work.tile([P, 4, P], F32, name="one", bufs=4)
                copy = nc.vector.tensor_copy if (u == UNITS - 1 and j == 1) else nc.scalar.copy
                copy(out=one[:], in_=obank[u, j][:])
                b, i0 = u // PER_BATCH, TILES * (u % PER_BATCH) + j
                nc.sync.dma_start(out=out[b].rearrange("h (p i) d -> p h i d", i=ROWS)[:, :, i0, :], in_=one[:])
                return
            left[n] = left.get(n, STORE * TILES) - 1
            if n not in outs:
                stage = work.tile([P, 4, STORE * TILES, P], F32, name="stage", bufs=3)
                outs[n] = stage
            nc.scalar.copy(out=outs[n][:, :, (u % STORE) * TILES + j, :], in_=obank[u, j][:])
            if left[n] == 0:
                b, i0 = n * STORE // PER_BATCH, TILES * (n * STORE % PER_BATCH)
                dst = out[b].rearrange("h (p i) d -> p h i d", i=ROWS)[:, :, i0 : i0 + STORE * TILES, :]
                nc.sync.dma_start(
                    out=dst.rearrange("p h i d -> p h (i d)"), in_=outs[n][:].rearrange("p h i d -> p h (i d)")
                )

        def tables(u):
            if u >= PER_BATCH:
                return
            bank = psum.tile([P, 2, TILES, P], BF16, name="bank", bufs=BANKS)
            for j in range(TILES):
                nc.tensor.transpose(bank[:, 0, j, :], rope_c[:, u * TILES + j, :], ident_b[:])
                nc.tensor.transpose(bank[:, 1, j, :], rope_s[:, u * TILES + j, :], ident_b[:])
            cols = slice(u * TOK, (u + 1) * TOK)
            nc.scalar.copy(out=tabs[:, 1:3, cols], in_=bank[:].rearrange("p a j r -> p a (j r)"))
            nc.scalar.activation(
                out=tabs[:, 0, cols], in_=bank[:, 1].rearrange("p j r -> p (j r)"), func=ACT.Copy, scale=-1.0
            )

        nc.vector.tensor_copy(
            out=wd[:].bitcast(I32).rearrange("p (t m) -> p t m", t=4),
            in_=wd_raw[:].bitcast(I32).rearrange("p (m t) -> p t m", t=4),
        )
        nc.vector.tensor_copy(
            out=wdsc[:].rearrange("p (t m) -> p m t", t=4), in_=wsc_raw[:, 0:LAT].rearrange("p (m t) -> p m t", t=4)
        )
        nc.vector.tensor_copy(out=bd[:], in_=bd_b[:])
        nc.vector.tensor_copy(out=bu[:], in_=bu_b[:])

        order = [
            (lambda u: leave_out(u, 1), 1, 7),
            (turn_x, 1, 2),
            (products, 1, 6),
            (lambda u: leave_out(u, 0), 0, 6),
            (lambda u: leave_down(u, 0), 1, 5),
            (lambda u: leave_down(u, 0), 0, 4),
            (lambda u: leave_out(u, 1), 0, 6),
            (tables, 0, 3),
            (tables, 1, 3),
            (turn_x, 0, 1),
            (cast, 1, 1),
            (lambda u: down(u, 0), 0, 3),
            (quant, 1, 3),
            (up, 1, 5),
            (lambda u: down(u, 1), 0, 3),
            (products, 0, 5),
            (quant, 0, 2),
            (scale_x, 1, 2),
            (up, 0, 4),
            (bias_up, 1, 5),
            (lambda u: down(u, 1), 1, 3),
            (lambda u: leave_down(u, 1), 0, 3),
            (lambda u: leave_down(u, 1), 1, 4),
            (bias_up, 0, 4),
            (mix, 0, 5),
            (cast, 0, 0),
            (lambda u: down(u, 0), 1, 4),
            (lambda u: turn_out(u, 0), 1, 6),
            (scale_x, 0, 1),
            (lambda u: turn_out(u, 1), 1, 6),
            (mix, 1, 5),
            (lambda u: turn_out(u, 0), 0, 5),
            (lambda u: turn_out(u, 1), 0, 5),
            (lambda u: leave_out(u, 0), 1, 6),
        ]
        for s in range((UNITS + D) // MU + 7 + 1):
            for stage, r, lag in order:
                u = MU * (s - lag) + r
                if 0 <= u < UNITS + (D if stage is quant else 0):
                    stage(u)
